import numpy as np
import ml_dtypes


def mxq(x, axis, fmt="e4m3"):
    dtype, down = {"e4m3": (ml_dtypes.float8_e4m3fn, 7), "e5m2": (ml_dtypes.float8_e5m2, 14)}[fmt]
    v = np.moveaxis(np.asarray(x, np.float32).astype(ml_dtypes.bfloat16).astype(np.float64), axis, -1)
    blocks = v.reshape(v.shape[:-1] + (-1, 32))
    amax = np.abs(blocks).max(-1, keepdims=True)
    byte = np.maximum(np.where(amax > 0, np.frexp(amax)[1] - 1 + 127, 0) - down, 1)
    scale = np.exp2(byte - 127.0)
    codes = (blocks / scale).astype(np.float32).astype(dtype).astype(np.float64)
    return np.moveaxis((codes * scale).reshape(v.shape), -1, axis)


WIDE = False


def mx_kscale(k):
    if not WIDE:
        return np.ones(k)
    levels = np.array([20, -20, 10, -10, 0])
    a = np.random.permutation(np.resize(levels, k // 512 * 4)).reshape(k // 512, 4)
    idx = np.arange(k)
    return np.exp2(a[idx // 512, idx % 128 // 32])


BF16 = ml_dtypes.bfloat16


def bf(x):
    return np.asarray(x, np.float32).astype(BF16)


def f64(x):
    return np.asarray(x).astype(np.float64)


C, G, P, E = 1024, 1024, 16, 192


def setup_inputs():
    s = mx_kscale(C)
    x = np.random.standard_normal((C, G)) * s[:, None]
    mask = np.random.randint(0, 2, (G, P))
    W = np.random.standard_normal((G, P * E)) * 1.4 / np.sqrt(G)
    b = np.random.standard_normal(P * E) * 0.3
    g = np.random.standard_normal((C, P, E)) * np.exp2(np.random.randint(-12, 1, (C, 1, 1))) / s[:, None, None]
    return {"x": bf(x), "mask": bf(mask), "W": bf(W), "b": bf(b), "grad_out": bf(g)}


def reference(x, mask, W, b, grad_out):
    gy = f64(grad_out).transpose(0, 2, 1).reshape(C, E * P)
    mask_rep = np.repeat(f64(mask), E, axis=1)
    gWm = mxq(f64(x), 0, "e4m3").T @ mxq(gy, 0, "e5m2")
    return gWm * mask_rep

@@ -1,0 +1,173 @@
+from contextlib import ExitStack
+
+import concourse.bass as bass
+import concourse.mybir as mybir
+import concourse.tile as tile
+
+F32 = mybir.dt.float32
+BF16 = mybir.dt.bfloat16
+U32 = mybir.dt.uint32
+U8 = mybir.dt.uint8
+E4X4 = mybir.dt.float8_e4m3fn_x4
+E5X4 = mybir.dt.float8_e5m2_x4
+COPY = mybir.ActivationFunctionType.Copy
+MULT = mybir.AluOpType.mult
+
+C, G, NP, E = 1024, 1024, 16, 192
+J = NP * E
+P = 128
+PACK = 4
+K_PASS = P * PACK
+PASSES = C // K_PASS
+N_BANK = 512
+E_BANK = N_BANK // NP
+BANKS = J // N_BANK
+G_TILES = G // P
+E_MASK = J // NP // NP
+PC = 4
+CHUNKS = NP // PC
+XA = 256
+LEAD = 7
+HALF = 3
+
+FLOPS = 2 * C * G * J
+BYTES = 2 * C * G + 2 * C * J + 2 * G * NP + 4 * G * J
+
+EVAC_ON_VECTOR = (0, 1, 0, 1, 0, 0, 1, 0, 1, 0, 0, 1)
+
+
+def tile_featureembed_kernel(tc, x, mask, W, b, grad_out, out):
+    nc = tc.nc
+    with ExitStack() as ctx:
+        raw = ctx.enter_context(tc.tile_pool(name="raw", bufs=1))
+        keep = ctx.enter_context(tc.tile_pool(name="keep", bufs=1))
+        grp = ctx.enter_context(tc.tile_pool(name="grp", bufs=4))
+        outp = ctx.enter_context(tc.tile_pool(name="outp", bufs=8))
+        psum = ctx.enter_context(tc.psum_pool(name="psum", bufs=8))
+
+        x_codes = keep.tile([P, PASSES, G], U32, align_bytes=64)
+        x_scales = keep.tile([P, PASSES, G], U8, align_bytes=64)
+        g_codes = keep.tile([P, PASSES, J], U32, align_bytes=64)
+        g_scales = keep.tile([P, PASSES, J], U8, align_bytes=64)
+        mask_bf = keep.tile([P, G_TILES, NP], BF16)
+        mask_f = keep.tile([P, G_TILES * NP], F32)
+
+        x_raw = []
+        for c in range(PASSES):
+            xr = raw.tile([P, PACK, G], BF16, name="x_raw%d" % c)
+            x_raw.append(xr)
+        g_raw = {}
+        for c in range(PASSES):
+            for q in range(CHUNKS):
+                gr = raw.tile([P, PACK, PC * E], BF16, name="g_raw%d_%d" % (c, q))
+                g_raw[(c, q)] = gr
+
+        def load_x(c, g0, g1):
+            rows = x[c * K_PASS : (c + 1) * K_PASS, g0:g1]
+            nc.sync.dma_start(out=x_raw[c][:, :, g0:g1], in_=rows.rearrange("(q j) g -> q j g", j=PACK))
+
+        for c in range(PASSES):
+            load_x(c, 0, XA)
+        for c in range(PASSES):
+            for q in range(CHUNKS):
+                rows = grad_out[c * K_PASS : (c + 1) * K_PASS, q * PC : (q + 1) * PC, :]
+                nc.sync.dma_start(out=g_raw[(c, q)][:], in_=rows.rearrange("(q j) p e -> q j (p e)", j=PACK))
+        nc.sync.dma_start(out=mask_bf[:], in_=mask.rearrange("(t q) m -> q t m", q=P))
+        for c in range(PASSES):
+            load_x(c, XA, G)
+
+        def prepare_x(c, piece, on_vector):
+            g0 = piece * XA
+            xg = grp.tile([P, XA, PACK], BF16, name="xg", align_bytes=64)
+            dst = xg[:].rearrange("q (n i) j -> q n j i", i=4)
+            src = x_raw[c][:, :, g0 : g0 + XA].rearrange("q j (n i) -> q n j i", i=4)
+            if on_vector:
+                nc.vector.tensor_copy(out=dst, in_=src)
+            else:
+                nc.scalar.copy(out=dst, in_=src)
+            nc.vector.quantize_mx(
+                out=x_codes[:, c, g0 : g0 + XA].bitcast(E4X4),
+                scales=x_scales[:, c, g0 : g0 + XA],
+                in_=xg[:].rearrange("q g j -> q (g j)"),
+            )
+
+        prepare_x(0, 0, True)
+        prepare_x(1, 0, False)
+
+        for c in range(PASSES):
+            for q in range(CHUNKS):
+                gg = grp.tile([P, BANKS, PC, E_BANK, PACK], BF16, name="gg", align_bytes=64)
+                for pl in range(PC):
+                    src = g_raw[(c, q)][:, :, pl * E : (pl + 1) * E]
+                    dst = gg[:, :, pl, :, :]
+                    if pl < PC // 2:
+                        nc.vector.tensor_copy(
+                            out=dst.rearrange("q b (n i) j -> q b n j i", i=4),
+                            in_=src.rearrange("q j (b n i) -> q b n j i", b=BANKS, i=4),
+                        )
+                    else:
+                        nc.scalar.copy(out=dst, in_=src.rearrange("q j (b e) -> q b e j", b=BANKS))
+                for eb in range(BANKS):
+                    c0 = eb * N_BANK + q * PC * E_BANK
+                    nc.vector.quantize_mx(
+                        out=g_codes[:, c, c0 : c0 + PC * E_BANK].bitcast(E5X4),
+                        scales=g_scales[:, c, c0 : c0 + PC * E_BANK],
+                        in_=gg[:, eb, :, :, :].rearrange("q p e j -> q (p e j)"),
+                    )
+
+        nc.scalar.copy(out=mask_f[:], in_=mask_bf[:].rearrange("q t m -> q (t m)"))
+
+        for piece in range(1, G // XA):
+            for c in range(PASSES):
+                prepare_x(c, piece, True)
+
+        accs = {}
+        outs = {}
+
+        def mx_pass(n, c):
+            t, eb = divmod(n, BANKS)
+            if c == 0:
+                acc = psum.tile([P, N_BANK], F32, name="acc")
+                accs[n] = acc
+            nc.tensor.matmul_mx(
+                out=accs[n][:],
+                lhsT=x_codes[:, c, t * P : (t + 1) * P].bitcast(E4X4),
+                lhsT_scale=x_scales[:, c, t * P : (t + 1) * P],
+                rhs=g_codes[:, c, eb * N_BANK : (eb + 1) * N_BANK].bitcast(E5X4),
+                rhs_scale=g_scales[:, c, eb * N_BANK : (eb + 1) * N_BANK],
+                start=(c == 0),
+                stop=(c == PASSES - 1),
+            )
+
+        def empty_bank(n):
+            t, eb = divmod(n, BANKS)
+            h, k = divmod(eb, HALF)
+            if k == 0:
+                ot = outp.tile([P, HALF * N_BANK], F32, name="ot")
+                outs[(t, h)] = ot
+            ot = outs[(t, h)]
+            bank = accs[n][:].rearrange("q (p e) -> q e p", p=NP)
+            e0 = eb * E_BANK
+            for m in range(e0 // E_MASK, (e0 + E_BANK - 1) // E_MASK + 1):
+                ea = max(e0, m * E_MASK)
+                ez = min(e0 + E_BANK, (m + 1) * E_MASK)
+                dst = ot[:, (ea - h * HALF * E_BANK) * NP : (ez - h * HALF * E_BANK) * NP]
+                dst = dst.rearrange("q (e p) -> q e p", p=NP)
+                src = bank[:, ea - e0 : ez - e0, :]
+                col = mask_f[:, t * NP + m : t * NP + m + 1]
+                if EVAC_ON_VECTOR[n % 12]:
+                    nc.vector.tensor_scalar(out=dst, in0=src, scalar1=col, scalar2=None, op0=MULT)
+                else:
+                    nc.scalar.activation(out=dst, in_=src, func=COPY, scale=col)
+            if k == HALF - 1:
+                nc.sync.dma_start(
+                    out=out[t * P : (t + 1) * P, h * HALF * N_BANK : (h + 1) * HALF * N_BANK], in_=ot[:]
+                )
+
+        total = G_TILES * BANKS
+        for n in range(total + LEAD):
+            if n < total:
+                mx_pass(n, 0)
+            if n >= LEAD:
+                mx_pass(n - LEAD, 1)
+                empty_bank(n - LEAD)

@@ -1,8 +1,6 @@
 from contextlib import ExitStack
 
-import concourse.bass as bass
 import concourse.mybir as mybir
-import concourse.tile as tile
 
 F32 = mybir.dt.float32
 BF16 = mybir.dt.bfloat16
@@ -23,17 +21,18 @@ N_BANK = 512
 E_BANK = N_BANK // NP
 BANKS = J // N_BANK
 G_TILES = G // P
-E_MASK = J // NP // NP
+E_MASK = E // NP
 PC = 4
 CHUNKS = NP // PC
 XA = 256
-LEAD = 7
 HALF = 3
+PSUM_BANKS = 8
+AHEAD = 4
+OUT_BUFS = 8
+X_PARTS = ((0, XA), (XA, G))
 
 FLOPS = 2 * C * G * J
 BYTES = 2 * C * G + 2 * C * J + 2 * G * NP + 4 * G * J
-
-EVAC_ON_VECTOR = (0, 1, 0, 1, 0, 0, 1, 0, 1, 0, 0, 1)
 
 
 def tile_featureembed_kernel(tc, x, mask, W, b, grad_out, out):
@@ -41,93 +40,103 @@ def tile_featureembed_kernel(tc, x, mask, W, b, grad_out, out):
     with ExitStack() as ctx:
         raw = ctx.enter_context(tc.tile_pool(name="raw", bufs=1))
         keep = ctx.enter_context(tc.tile_pool(name="keep", bufs=1))
-        grp = ctx.enter_context(tc.tile_pool(name="grp", bufs=4))
-        outp = ctx.enter_context(tc.tile_pool(name="outp", bufs=8))
-        psum = ctx.enter_context(tc.psum_pool(name="psum", bufs=8))
+        grp = ctx.enter_context(tc.tile_pool(name="grp", bufs=1))
+        outp = ctx.enter_context(tc.tile_pool(name="outp", bufs=1))
+        psum = ctx.enter_context(tc.psum_pool(name="psum", bufs=1))
+        ctx.enter_context(tc.manual_schedule())
 
         x_codes = keep.tile([P, PASSES, G], U32, align_bytes=64)
         x_scales = keep.tile([P, PASSES, G], U8, align_bytes=64)
         g_codes = keep.tile([P, PASSES, J], U32, align_bytes=64)
         g_scales = keep.tile([P, PASSES, J], U8, align_bytes=64)
         mask_bf = keep.tile([P, G_TILES, NP], BF16)
-        mask_f = keep.tile([P, G_TILES * NP], F32)
+        mask_e = keep.tile([P, G_TILES, E], F32)
 
-        x_raw = []
+        x_raw = {}
         for c in range(PASSES):
-            xr = raw.tile([P, PACK, G], BF16, name="x_raw%d" % c)
-            x_raw.append(xr)
-        g_raw = {}
-        for c in range(PASSES):
-            for q in range(CHUNKS):
-                gr = raw.tile([P, PACK, PC * E], BF16, name="g_raw%d_%d" % (c, q))
-                g_raw[(c, q)] = gr
+            for g0, g1 in X_PARTS:
+                xr = raw.tile([P, PACK, g1 - g0], BF16, name="x_raw%d_%d" % (c, g0))
+                x_raw[(c, g0)] = xr
+        g_raw = []
+        for i in range(PASSES * CHUNKS):
+            gr = raw.tile([P, PACK, PC * E], BF16, name="g_raw%d" % i)
+            g_raw.append(gr)
 
         def load_x(c, g0, g1):
             rows = x[c * K_PASS : (c + 1) * K_PASS, g0:g1]
-            nc.sync.dma_start(out=x_raw[c][:, :, g0:g1], in_=rows.rearrange("(q j) g -> q j g", j=PACK))
+            nc.sync.dma_start(out=x_raw[(c, g0)][:], in_=rows.rearrange("(q j) g -> q j g", j=PACK))
 
+        nc.scalar.dma_start(out=mask_bf[:], in_=mask.rearrange("(t q) m -> q t m", q=P))
         for c in range(PASSES):
             load_x(c, 0, XA)
-        for c in range(PASSES):
-            for q in range(CHUNKS):
-                rows = grad_out[c * K_PASS : (c + 1) * K_PASS, q * PC : (q + 1) * PC, :]
-                nc.sync.dma_start(out=g_raw[(c, q)][:], in_=rows.rearrange("(q j) p e -> q j (p e)", j=PACK))
-        nc.sync.dma_start(out=mask_bf[:], in_=mask.rearrange("(t q) m -> q t m", q=P))
+        for i in range(PASSES * CHUNKS):
+            c, q = divmod(i, CHUNKS)
+            rows = grad_out[c * K_PASS : (c + 1) * K_PASS, q * PC : (q + 1) * PC, :]
+            nc.sync.dma_start(out=g_raw[i][:], in_=rows.rearrange("(q j) p e -> q j (p e)", j=PACK))
         for c in range(PASSES):
             load_x(c, XA, G)
 
-        def prepare_x(c, piece, on_vector):
+        nc.scalar.copy(
+            out=mask_e[:].rearrange("q t (m r) -> q (t m) r", r=E_MASK),
+            in_=mask_bf[:].rearrange("q t m -> q (t m)").unsqueeze(2).to_broadcast([P, G_TILES * NP, E_MASK]),
+        )
+
+        xgs = {}
+
+        def copy_x(c, piece):
             g0 = piece * XA
-            xg = grp.tile([P, XA, PACK], BF16, name="xg", align_bytes=64)
-            dst = xg[:].rearrange("q (n i) j -> q n j i", i=4)
-            src = x_raw[c][:, :, g0 : g0 + XA].rearrange("q j (n i) -> q n j i", i=4)
-            if on_vector:
-                nc.vector.tensor_copy(out=dst, in_=src)
-            else:
-                nc.scalar.copy(out=dst, in_=src)
+            xg = grp.tile([P, XA, PACK], BF16, name="xg%d" % ((2 * piece + c) % 4), align_bytes=64)
+            xgs[(c, piece)] = xg
+            base = 0 if piece == 0 else XA
+            part = x_raw[(c, base)]
+            nc.vector.tensor_copy(
+                out=xg[:].rearrange("q (n i) j -> q n j i", i=4),
+                in_=part[:, :, g0 - base : g0 - base + XA].rearrange("q j (n i) -> q n j i", i=4),
+            )
+
+        def quantise_x(c, piece):
+            g0 = piece * XA
             nc.vector.quantize_mx(
                 out=x_codes[:, c, g0 : g0 + XA].bitcast(E4X4),
                 scales=x_scales[:, c, g0 : g0 + XA],
-                in_=xg[:].rearrange("q g j -> q (g j)"),
+                in_=xgs[(c, piece)][:].rearrange("q g j -> q (g j)"),
             )
 
-        prepare_x(0, 0, True)
-        prepare_x(1, 0, False)
+        ggs = {}
 
-        for c in range(PASSES):
-            for q in range(CHUNKS):
-                gg = grp.tile([P, BANKS, PC, E_BANK, PACK], BF16, name="gg", align_bytes=64)
-                for pl in range(PC):
-                    src = g_raw[(c, q)][:, :, pl * E : (pl + 1) * E]
-                    dst = gg[:, :, pl, :, :]
-                    if pl < PC // 2:
-                        nc.vector.tensor_copy(
-                            out=dst.rearrange("q b (n i) j -> q b n j i", i=4),
-                            in_=src.rearrange("q j (b n i) -> q b n j i", b=BANKS, i=4),
-                        )
-                    else:
-                        nc.scalar.copy(out=dst, in_=src.rearrange("q j (b e) -> q b e j", b=BANKS))
-                for eb in range(BANKS):
-                    c0 = eb * N_BANK + q * PC * E_BANK
-                    nc.vector.quantize_mx(
-                        out=g_codes[:, c, c0 : c0 + PC * E_BANK].bitcast(E5X4),
-                        scales=g_scales[:, c, c0 : c0 + PC * E_BANK],
-                        in_=gg[:, eb, :, :, :].rearrange("q p e j -> q (p e j)"),
+        def copy_g(i):
+            gg = grp.tile([P, BANKS, PC, E_BANK, PACK], BF16, name="gg%d" % i, align_bytes=64)
+            ggs[i] = gg
+            rows = g_raw[i][:].rearrange("q j (p e) -> q j p e", p=PC)
+            for eb in range(BANKS):
+                src = rows[:, :, :, eb * E_BANK : (eb + 1) * E_BANK]
+                dst = gg[:, eb, :, :, :]
+                if eb % 2 == 0:
+                    nc.vector.tensor_copy(
+                        out=dst.rearrange("q p (n i) j -> q p n j i", i=4),
+                        in_=src.rearrange("q j p (n i) -> q p n j i", i=4),
                     )
+                else:
+                    nc.scalar.copy(out=dst, in_=src.rearrange("q j p e -> q p e j"))
 
-        nc.scalar.copy(out=mask_f[:], in_=mask_bf[:].rearrange("q t m -> q (t m)"))
-
-        for piece in range(1, G // XA):
-            for c in range(PASSES):
-                prepare_x(c, piece, True)
+        def quantise_g(i):
+            c, q = divmod(i, CHUNKS)
+            for eb in range(BANKS):
+                c0 = eb * N_BANK + q * PC * E_BANK
+                nc.vector.quantize_mx(
+                    out=g_codes[:, c, c0 : c0 + PC * E_BANK].bitcast(E5X4),
+                    scales=g_scales[:, c, c0 : c0 + PC * E_BANK],
+                    in_=ggs[i][:, eb, :, :, :].rearrange("q p e j -> q (p e j)"),
+                )
 
         accs = {}
         outs = {}
+        total = G_TILES * BANKS
 
         def mx_pass(n, c):
             t, eb = divmod(n, BANKS)
             if c == 0:
-                acc = psum.tile([P, N_BANK], F32, name="acc")
+                acc = psum.tile([P, N_BANK], F32, name="acc%d" % (n % PSUM_BANKS))
                 accs[n] = acc
             nc.tensor.matmul_mx(
                 out=accs[n][:],
@@ -142,32 +151,62 @@ def tile_featureembed_kernel(tc, x, mask, W, b, grad_out, out):
         def empty_bank(n):
             t, eb = divmod(n, BANKS)
             h, k = divmod(eb, HALF)
+            u = t * (BANKS // HALF) + h
             if k == 0:
-                ot = outp.tile([P, HALF * N_BANK], F32, name="ot")
-                outs[(t, h)] = ot
-            ot = outs[(t, h)]
+                ot = outp.tile([P, HALF * N_BANK], F32, name="ot%d" % (u % OUT_BUFS))
+                outs[u] = ot
+            ot = outs[u]
             bank = accs[n][:].rearrange("q (p e) -> q e p", p=NP)
             e0 = eb * E_BANK
-            for m in range(e0 // E_MASK, (e0 + E_BANK - 1) // E_MASK + 1):
-                ea = max(e0, m * E_MASK)
-                ez = min(e0 + E_BANK, (m + 1) * E_MASK)
-                dst = ot[:, (ea - h * HALF * E_BANK) * NP : (ez - h * HALF * E_BANK) * NP]
-                dst = dst.rearrange("q (e p) -> q e p", p=NP)
-                src = bank[:, ea - e0 : ez - e0, :]
-                col = mask_f[:, t * NP + m : t * NP + m + 1]
-                if EVAC_ON_VECTOR[n % 12]:
-                    nc.vector.tensor_scalar(out=dst, in0=src, scalar1=col, scalar2=None, op0=MULT)
-                else:
-                    nc.scalar.activation(out=dst, in_=src, func=COPY, scale=col)
-            if k == HALF - 1:
-                nc.sync.dma_start(
-                    out=out[t * P : (t + 1) * P, h * HALF * N_BANK : (h + 1) * HALF * N_BANK], in_=ot[:]
+            if n % 2 == 1:
+                nc.vector.tensor_tensor(
+                    out=ot[:, k * N_BANK : (k + 1) * N_BANK].rearrange("q (e p) -> q e p", p=NP),
+                    in0=bank,
+                    in1=mask_e[:, t, e0 : e0 + E_BANK].unsqueeze(2).to_broadcast([P, E_BANK, NP]),
+                    op=MULT,
                 )
+            else:
+                for m in range(e0 // E_MASK, (e0 + E_BANK - 1) // E_MASK + 1):
+                    ea = max(e0, m * E_MASK)
+                    ez = min(e0 + E_BANK, (m + 1) * E_MASK)
+                    dst = ot[:, (ea - h * HALF * E_BANK) * NP : (ez - h * HALF * E_BANK) * NP]
+                    nc.scalar.activation(
+                        out=dst.rearrange("q (e p) -> q e p", p=NP),
+                        in_=bank[:, ea - e0 : ez - e0, :],
+                        func=COPY,
+                        scale=mask_e[:, t, m * E_MASK : m * E_MASK + 1],
+                    )
+            rows = out[t * P : (t + 1) * P, :]
+            if u == G_TILES * (BANKS // HALF) - 1:
+                nc.sync.dma_start(
+                    out=rows[:, eb * N_BANK : (eb + 1) * N_BANK], in_=ot[:, k * N_BANK : (k + 1) * N_BANK]
+                )
+            elif k == HALF - 1:
+                nc.sync.dma_start(out=rows[:, h * HALF * N_BANK : (h + 1) * HALF * N_BANK], in_=ot[:])
 
-        total = G_TILES * BANKS
-        for n in range(total + LEAD):
-            if n < total:
-                mx_pass(n, 0)
-            if n >= LEAD:
-                mx_pass(n - LEAD, 1)
-                empty_bank(n - LEAD)
+        copy_x(0, 0)
+        copy_x(1, 0)
+        quantise_x(0, 0)
+        quantise_x(1, 0)
+        for i in range(PASSES * CHUNKS):
+            copy_g(i)
+            if i > 0:
+                quantise_g(i - 1)
+            if i == CHUNKS:
+                for n in range(PSUM_BANKS):
+                    mx_pass(n, 0)
+        quantise_g(PASSES * CHUNKS - 1)
+
+        for n in range(total):
+            mx_pass(n, 1)
+            empty_bank(n)
+            if PSUM_BANKS <= n + AHEAD < total:
+                mx_pass(n + AHEAD, 0)
+            piece = n // (2 * BANKS) + 1
+            if piece < G // XA:
+                if n % (2 * BANKS) == 3:
+                    copy_x(0, piece)
+                    quantise_x(0, piece)
+                if n % (2 * BANKS) == 7:
+                    copy_x(1, piece)
+                    quantise_x(1, piece)

@@ -30,6 +30,7 @@ PSUM_BANKS = 8
 AHEAD = 4
 OUT_BUFS = 8
 X_PARTS = ((0, XA), (XA, G))
+STORE_CUTS = {0: (0, 1, 3), 15: (0, 1, 2, 3)}
 
 FLOPS = 2 * C * G * J
 BYTES = 2 * C * G + 2 * C * J + 2 * G * NP + 4 * G * J
@@ -67,12 +68,13 @@ def tile_featureembed_kernel(tc, x, mask, W, b, grad_out, out):
             nc.sync.dma_start(out=x_raw[(c, g0)][:], in_=rows.rearrange("(q j) g -> q j g", j=PACK))
 
         nc.scalar.dma_start(out=mask_bf[:], in_=mask.rearrange("(t q) m -> q t m", q=P))
-        for c in range(PASSES):
-            load_x(c, 0, XA)
         for i in range(PASSES * CHUNKS):
             c, q = divmod(i, CHUNKS)
             rows = grad_out[c * K_PASS : (c + 1) * K_PASS, q * PC : (q + 1) * PC, :]
             nc.sync.dma_start(out=g_raw[i][:], in_=rows.rearrange("(q j) p e -> q j (p e)", j=PACK))
+            if i == 0:
+                for c in range(PASSES):
+                    load_x(c, 0, XA)
         for c in range(PASSES):
             load_x(c, XA, G)
 
@@ -104,30 +106,29 @@ def tile_featureembed_kernel(tc, x, mask, W, b, grad_out, out):
 
         ggs = {}
 
-        def copy_g(i):
-            gg = grp.tile([P, BANKS, PC, E_BANK, PACK], BF16, name="gg%d" % i, align_bytes=64)
-            ggs[i] = gg
+        def copy_g(i, eb):
+            if i not in ggs:
+                gg = grp.tile([P, BANKS, PC, E_BANK, PACK], BF16, name="gg%d" % i, align_bytes=64)
+                ggs[i] = gg
             rows = g_raw[i][:].rearrange("q j (p e) -> q j p e", p=PC)
-            for eb in range(BANKS):
-                src = rows[:, :, :, eb * E_BANK : (eb + 1) * E_BANK]
-                dst = gg[:, eb, :, :, :]
-                if eb % 2 == 0:
-                    nc.vector.tensor_copy(
-                        out=dst.rearrange("q p (n i) j -> q p n j i", i=4),
-                        in_=src.rearrange("q j p (n i) -> q p n j i", i=4),
-                    )
-                else:
-                    nc.scalar.copy(out=dst, in_=src.rearrange("q j p e -> q p e j"))
-
-        def quantise_g(i):
-            c, q = divmod(i, CHUNKS)
-            for eb in range(BANKS):
-                c0 = eb * N_BANK + q * PC * E_BANK
-                nc.vector.quantize_mx(
-                    out=g_codes[:, c, c0 : c0 + PC * E_BANK].bitcast(E5X4),
-                    scales=g_scales[:, c, c0 : c0 + PC * E_BANK],
-                    in_=ggs[i][:, eb, :, :, :].rearrange("q p e j -> q (p e j)"),
+            src = rows[:, :, :, eb * E_BANK : (eb + 1) * E_BANK]
+            dst = ggs[i][:, eb, :, :, :]
+            if eb % 2 == 0:
+                nc.vector.tensor_copy(
+                    out=dst.rearrange("q p (n i) j -> q p n j i", i=4),
+                    in_=src.rearrange("q j p (n i) -> q p n j i", i=4),
                 )
+            else:
+                nc.scalar.copy(out=dst, in_=src.rearrange("q j p e -> q p e j"))
+
+        def quantise_g(i, eb):
+            c, q = divmod(i, CHUNKS)
+            c0 = eb * N_BANK + q * PC * E_BANK
+            nc.vector.quantize_mx(
+                out=g_codes[:, c, c0 : c0 + PC * E_BANK].bitcast(E5X4),
+                scales=g_scales[:, c, c0 : c0 + PC * E_BANK],
+                in_=ggs[i][:, eb, :, :, :].rearrange("q p e j -> q (p e j)"),
+            )
 
         accs = {}
         outs = {}
@@ -176,26 +177,47 @@ def tile_featureembed_kernel(tc, x, mask, W, b, grad_out, out):
                         func=COPY,
                         scale=mask_e[:, t, m * E_MASK : m * E_MASK + 1],
                     )
-            rows = out[t * P : (t + 1) * P, :]
-            if u == G_TILES * (BANKS // HALF) - 1:
+            rows = out[t * P : (t + 1) * P, h * HALF * N_BANK : (h + 1) * HALF * N_BANK]
+            cuts = STORE_CUTS.get(u, (0, HALF))
+            if k + 1 in cuts:
+                k0 = cuts[cuts.index(k + 1) - 1]
                 nc.sync.dma_start(
-                    out=rows[:, eb * N_BANK : (eb + 1) * N_BANK], in_=ot[:, k * N_BANK : (k + 1) * N_BANK]
+                    out=rows[:, k0 * N_BANK : (k + 1) * N_BANK], in_=ot[:, k0 * N_BANK : (k + 1) * N_BANK]
                 )
-            elif k == HALF - 1:
-                nc.sync.dma_start(out=rows[:, h * HALF * N_BANK : (h + 1) * HALF * N_BANK], in_=ot[:])
 
-        copy_x(0, 0)
-        copy_x(1, 0)
-        quantise_x(0, 0)
-        quantise_x(1, 0)
-        for i in range(PASSES * CHUNKS):
-            copy_g(i)
-            if i > 0:
-                quantise_g(i - 1)
+        last = PASSES * CHUNKS - 1
+        for i in range(last + 1):
+            for eb in (1, 3, 5):
+                copy_g(i, eb)
+            if i < last:
+                for eb in (0, 2, 4):
+                    copy_g(i, eb)
+                    if i > 0:
+                        quantise_g(i - 1, eb + 1)
+                if i == 0:
+                    copy_x(0, 0)
+                    copy_x(1, 0)
+                for eb in (0, 2, 4):
+                    quantise_g(i, eb)
+                if i == 0:
+                    quantise_x(0, 0)
+                    quantise_x(1, 0)
+            else:
+                copy_g(i, 0)
+                quantise_g(i - 1, 1)
+                quantise_g(i, 0)
+                copy_g(i, 2)
+                quantise_g(i, 1)
+                quantise_g(i - 1, 3)
+                quantise_g(i, 2)
+                copy_g(i, 4)
+                quantise_g(i, 3)
+                quantise_g(i - 1, 5)
+                quantise_g(i, 4)
+                quantise_g(i, 5)
             if i == CHUNKS:
                 for n in range(PSUM_BANKS):
                     mx_pass(n, 0)
-        quantise_g(PASSES * CHUNKS - 1)
 
         for n in range(total):
             mx_pass(n, 1)

@@ -31,6 +31,8 @@ AHEAD = 4
 OUT_BUFS = 8
 X_PARTS = ((0, XA), (XA, G))
 STORE_CUTS = {0: (0, 1, 3), 15: (0, 1, 2, 3)}
+CHUNK_ORDER = ((0, 0), (0, 1), (0, 2), (1, 0), (0, 3), (1, 1), (1, 2), (1, 3))
+HEAD_START_AFTER = 5
 
 FLOPS = 2 * C * G * J
 BYTES = 2 * C * G + 2 * C * J + 2 * G * NP + 4 * G * J
@@ -69,7 +71,7 @@ def tile_featureembed_kernel(tc, x, mask, W, b, grad_out, out):
 
         nc.scalar.dma_start(out=mask_bf[:], in_=mask.rearrange("(t q) m -> q t m", q=P))
         for i in range(PASSES * CHUNKS):
-            c, q = divmod(i, CHUNKS)
+            c, q = CHUNK_ORDER[i]
             rows = grad_out[c * K_PASS : (c + 1) * K_PASS, q * PC : (q + 1) * PC, :]
             nc.sync.dma_start(out=g_raw[i][:], in_=rows.rearrange("(q j) p e -> q j (p e)", j=PACK))
             if i == 0:
@@ -122,7 +124,7 @@ def tile_featureembed_kernel(tc, x, mask, W, b, grad_out, out):
                 nc.scalar.copy(out=dst, in_=src.rearrange("q j p e -> q p e j"))
 
         def quantise_g(i, eb):
-            c, q = divmod(i, CHUNKS)
+            c, q = CHUNK_ORDER[i]
             c0 = eb * N_BANK + q * PC * E_BANK
             nc.vector.quantize_mx(
                 out=g_codes[:, c, c0 : c0 + PC * E_BANK].bitcast(E5X4),
@@ -215,7 +217,7 @@ def tile_featureembed_kernel(tc, x, mask, W, b, grad_out, out):
                 quantise_g(i - 1, 5)
                 quantise_g(i, 4)
                 quantise_g(i, 5)
-            if i == CHUNKS:
+            if i == HEAD_START_AFTER:
                 for n in range(PSUM_BANKS):
                     mx_pass(n, 0)
 

@@ -52,8 +52,13 @@ def tile_featureembed_kernel(tc, x, mask, W, b, grad_out, out):
         x_scales = keep.tile([P, PASSES, G], U8, align_bytes=64)
         g_codes = keep.tile([P, PASSES, J], U32, align_bytes=64)
         g_scales = keep.tile([P, PASSES, J], U8, align_bytes=64)
-        mask_bf = keep.tile([P, G_TILES, NP], BF16)
-        mask_e = keep.tile([P, G_TILES, E], F32)
+        mask_bf = []
+        mask_e = []
+        for u in range(G // XA):
+            mb = keep.tile([P, XA // P, NP], BF16, name="mask_bf%d" % u)
+            me = keep.tile([P, XA // P, E], F32, name="mask_e%d" % u)
+            mask_bf.append(mb)
+            mask_e.append(me)
 
         x_raw = {}
         for c in range(PASSES):
@@ -69,21 +74,33 @@ def tile_featureembed_kernel(tc, x, mask, W, b, grad_out, out):
             rows = x[c * K_PASS : (c + 1) * K_PASS, g0:g1]
             nc.sync.dma_start(out=x_raw[(c, g0)][:], in_=rows.rearrange("(q j) g -> q j g", j=PACK))
 
-        nc.scalar.dma_start(out=mask_bf[:], in_=mask.rearrange("(t q) m -> q t m", q=P))
+        def load_mask(u):
+            rows = mask[u * XA : (u + 1) * XA, :]
+            nc.sync.dma_start(out=mask_bf[u][:], in_=rows.rearrange("(t q) m -> q t m", q=P))
+
+        def expand_mask(u):
+            nc.scalar.copy(
+                out=mask_e[u][:].rearrange("q t (m r) -> q (t m) r", r=E_MASK),
+                in_=mask_bf[u][:]
+                .rearrange("q t m -> q (t m)")
+                .unsqueeze(2)
+                .to_broadcast([P, XA // P * NP, E_MASK]),
+            )
+
         for i in range(PASSES * CHUNKS):
             c, q = CHUNK_ORDER[i]
             rows = grad_out[c * K_PASS : (c + 1) * K_PASS, q * PC : (q + 1) * PC, :]
             nc.sync.dma_start(out=g_raw[i][:], in_=rows.rearrange("(q j) p e -> q j (p e)", j=PACK))
             if i == 0:
+                load_mask(0)
                 for c in range(PASSES):
                     load_x(c, 0, XA)
-        for c in range(PASSES):
-            load_x(c, XA, G)
+        load_x(0, XA, G)
+        for u in range(1, G // XA):
+            load_mask(u)
+        load_x(1, XA, G)
 
-        nc.scalar.copy(
-            out=mask_e[:].rearrange("q t (m r) -> q (t m) r", r=E_MASK),
-            in_=mask_bf[:].rearrange("q t m -> q (t m)").unsqueeze(2).to_broadcast([P, G_TILES * NP, E_MASK]),
-        )
+        expand_mask(0)
 
         xgs = {}
 
@@ -165,7 +182,7 @@ def tile_featureembed_kernel(tc, x, mask, W, b, grad_out, out):
                 nc.vector.tensor_tensor(
                     out=ot[:, k * N_BANK : (k + 1) * N_BANK].rearrange("q (e p) -> q e p", p=NP),
                     in0=bank,
-                    in1=mask_e[:, t, e0 : e0 + E_BANK].unsqueeze(2).to_broadcast([P, E_BANK, NP]),
+                    in1=mask_e[t // 2][:, t % 2, e0 : e0 + E_BANK].unsqueeze(2).to_broadcast([P, E_BANK, NP]),
                     op=MULT,
                 )
             else:
@@ -177,7 +194,7 @@ def tile_featureembed_kernel(tc, x, mask, W, b, grad_out, out):
                         out=dst.rearrange("q (e p) -> q e p", p=NP),
                         in_=bank[:, ea - e0 : ez - e0, :],
                         func=COPY,
-                        scale=mask_e[:, t, m * E_MASK : m * E_MASK + 1],
+                        scale=mask_e[t // 2][:, t % 2, m * E_MASK : m * E_MASK + 1],
                     )
             rows = out[t * P : (t + 1) * P, h * HALF * N_BANK : (h + 1) * HALF * N_BANK]
             cuts = STORE_CUTS.get(u, (0, HALF))
@@ -228,6 +245,8 @@ def tile_featureembed_kernel(tc, x, mask, W, b, grad_out, out):
                 mx_pass(n + AHEAD, 0)
             piece = n // (2 * BANKS) + 1
             if piece < G // XA:
+                if n % (2 * BANKS) == 9:
+                    expand_mask(piece)
                 if n % (2 * BANKS) == 3:
                     copy_x(0, piece)
                     quantise_x(0, piece)

@@ -249,7 +249,9 @@ def tile_featureembed_kernel(tc, x, mask, W, b, grad_out, out):
                     expand_mask(piece)
                 if n % (2 * BANKS) == 3:
                     copy_x(0, piece)
+                if n % (2 * BANKS) == 5:
                     quantise_x(0, piece)
                 if n % (2 * BANKS) == 7:
                     copy_x(1, piece)
+                if n % (2 * BANKS) == 9:
                     quantise_x(1, piece)

@@ -200,7 +200,8 @@ def tile_featureembed_kernel(tc, x, mask, W, b, grad_out, out):
             cuts = STORE_CUTS.get(u, (0, HALF))
             if k + 1 in cuts:
                 k0 = cuts[cuts.index(k + 1) - 1]
-                nc.sync.dma_start(
+                queue = nc.scalar if h == 0 else nc.sync
+                queue.dma_start(
                     out=rows[:, k0 * N_BANK : (k + 1) * N_BANK], in_=ot[:, k0 * N_BANK : (k + 1) * N_BANK]
                 )
 

@@ -22,8 +22,6 @@ E_BANK = N_BANK // NP
 BANKS = J // N_BANK
 G_TILES = G // P
 E_MASK = E // NP
-PC = 4
-CHUNKS = NP // PC
 XA = 256
 HALF = 3
 PSUM_BANKS = 8
@@ -31,7 +29,8 @@ AHEAD = 4
 OUT_BUFS = 8
 X_PARTS = ((0, XA), (XA, G))
 STORE_CUTS = {0: (0, 1, 3), 15: (0, 1, 2, 3)}
-CHUNK_ORDER = ((0, 0), (0, 1), (0, 2), (1, 0), (0, 3), (1, 1), (1, 2), (1, 3))
+CHUNK_ORDER = ((0, 0, 4), (0, 4, 4), (0, 8, 4), (1, 0, 4), (0, 12, 4), (1, 4, 4), (1, 8, 4), (1, 12, 2), (1, 14, 2))
+N_CHUNKS = len(CHUNK_ORDER)
 HEAD_START_AFTER = 5
 
 FLOPS = 2 * C * G * J
@@ -66,8 +65,8 @@ def tile_featureembed_kernel(tc, x, mask, W, b, grad_out, out):
                 xr = raw.tile([P, PACK, g1 - g0], BF16, name="x_raw%d_%d" % (c, g0))
                 x_raw[(c, g0)] = xr
         g_raw = []
-        for i in range(PASSES * CHUNKS):
-            gr = raw.tile([P, PACK, PC * E], BF16, name="g_raw%d" % i)
+        for i in range(N_CHUNKS):
+            gr = raw.tile([P, PACK, CHUNK_ORDER[i][2] * E], BF16, name="g_raw%d" % i)
             g_raw.append(gr)
 
         def load_x(c, g0, g1):
@@ -87,9 +86,9 @@ def tile_featureembed_kernel(tc, x, mask, W, b, grad_out, out):
                 .to_broadcast([P, XA // P * NP, E_MASK]),
             )
 
-        for i in range(PASSES * CHUNKS):
-            c, q = CHUNK_ORDER[i]
-            rows = grad_out[c * K_PASS : (c + 1) * K_PASS, q * PC : (q + 1) * PC, :]
+        for i in range(N_CHUNKS):
+            c, p0, pn = CHUNK_ORDER[i]
+            rows = grad_out[c * K_PASS : (c + 1) * K_PASS, p0 : p0 + pn, :]
             nc.sync.dma_start(out=g_raw[i][:], in_=rows.rearrange("(q j) p e -> q j (p e)", j=PACK))
             if i == 0:
                 load_mask(0)
@@ -126,10 +125,11 @@ def tile_featureembed_kernel(tc, x, mask, W, b, grad_out, out):
         ggs = {}
 
         def copy_g(i, eb):
+            pn = CHUNK_ORDER[i][2]
             if i not in ggs:
-                gg = grp.tile([P, BANKS, PC, E_BANK, PACK], BF16, name="gg%d" % i, align_bytes=64)
+                gg = grp.tile([P, BANKS, pn, E_BANK, PACK], BF16, name="gg%d" % i, align_bytes=64)
                 ggs[i] = gg
-            rows = g_raw[i][:].rearrange("q j (p e) -> q j p e", p=PC)
+            rows = g_raw[i][:].rearrange("q j (p e) -> q j p e", p=pn)
             src = rows[:, :, :, eb * E_BANK : (eb + 1) * E_BANK]
             dst = ggs[i][:, eb, :, :, :]
             if eb % 2 == 0:
@@ -141,11 +141,11 @@ def tile_featureembed_kernel(tc, x, mask, W, b, grad_out, out):
                 nc.scalar.copy(out=dst, in_=src.rearrange("q j p e -> q p e j"))
 
         def quantise_g(i, eb):
-            c, q = CHUNK_ORDER[i]
-            c0 = eb * N_BANK + q * PC * E_BANK
+            c, p0, pn = CHUNK_ORDER[i]
+            c0 = eb * N_BANK + p0 * E_BANK
             nc.vector.quantize_mx(
-                out=g_codes[:, c, c0 : c0 + PC * E_BANK].bitcast(E5X4),
-                scales=g_scales[:, c, c0 : c0 + PC * E_BANK],
+                out=g_codes[:, c, c0 : c0 + pn * E_BANK].bitcast(E5X4),
+                scales=g_scales[:, c, c0 : c0 + pn * E_BANK],
                 in_=ggs[i][:, eb, :, :, :].rearrange("q p e j -> q (p e j)"),
             )
 
@@ -205,7 +205,7 @@ def tile_featureembed_kernel(tc, x, mask, W, b, grad_out, out):
                     out=rows[:, k0 * N_BANK : (k + 1) * N_BANK], in_=ot[:, k0 * N_BANK : (k + 1) * N_BANK]
                 )
 
-        last = PASSES * CHUNKS - 1
+        last = N_CHUNKS - 1
         for i in range(last + 1):
             for eb in (1, 3, 5):
                 copy_g(i, eb)

@@ -178,6 +178,21 @@ def tile_featureembed_kernel(tc, x, mask, W, b, grad_out, out):
             ot = outs[u]
             bank = accs[n][:].rearrange("q (p e) -> q e p", p=NP)
             e0 = eb * E_BANK
+            rows = out[t * P : (t + 1) * P, h * HALF * N_BANK : (h + 1) * HALF * N_BANK]
+            if n == total - 1:
+                ew = E_BANK // 2
+                for part, queue in enumerate((nc.scalar, nc.sync)):
+                    c0 = k * N_BANK + part * ew * NP
+                    nc.vector.tensor_tensor(
+                        out=ot[:, c0 : c0 + ew * NP].rearrange("q (e p) -> q e p", p=NP),
+                        in0=bank[:, part * ew : (part + 1) * ew, :],
+                        in1=mask_e[t // 2][:, t % 2, e0 + part * ew : e0 + (part + 1) * ew]
+                        .unsqueeze(2)
+                        .to_broadcast([P, ew, NP]),
+                        op=MULT,
+                    )
+                    queue.dma_start(out=rows[:, c0 : c0 + ew * NP], in_=ot[:, c0 : c0 + ew * NP])
+                return
             if n % 2 == 1:
                 nc.vector.tensor_tensor(
                     out=ot[:, k * N_BANK : (k + 1) * N_BANK].rearrange("q (e p) -> q e p", p=NP),
@@ -196,7 +211,6 @@ def tile_featureembed_kernel(tc, x, mask, W, b, grad_out, out):
                         func=COPY,
                         scale=mask_e[t // 2][:, t % 2, m * E_MASK : m * E_MASK + 1],
                     )
-            rows = out[t * P : (t + 1) * P, h * HALF * N_BANK : (h + 1) * HALF * N_BANK]
             cuts = STORE_CUTS.get(u, (0, HALF))
             if k + 1 in cuts:
                 k0 = cuts[cuts.index(k + 1) - 1]

@@ -28,10 +28,14 @@ PSUM_BANKS = 8
 AHEAD = 4
 OUT_BUFS = 8
 X_PARTS = ((0, XA), (XA, G))
-STORE_CUTS = {0: (0, 1, 3), 15: (0, 1, 2, 3)}
+STORE_CUTS = {0: (0, 1, 2, 3), 1: (0, 1, 2, 3), 15: (0, 1, 2, 3)}
 CHUNK_ORDER = ((0, 0, 4), (0, 4, 4), (0, 8, 4), (1, 0, 4), (0, 12, 4), (1, 4, 4), (1, 8, 4), (1, 12, 2), (1, 14, 2))
 N_CHUNKS = len(CHUNK_ORDER)
 HEAD_START_AFTER = 5
+HEAD_BANKS = PSUM_BANKS - 1
+WARM_CHUNKS = (6, 7)
+WARM_PER_CHUNK = 3
+WARM_COLS = 2 * E
 
 FLOPS = 2 * C * G * J
 BYTES = 2 * C * G + 2 * C * J + 2 * G * NP + 4 * G * J
@@ -168,6 +172,17 @@ def tile_featureembed_kernel(tc, x, mask, W, b, grad_out, out):
                 stop=(c == PASSES - 1),
             )
 
+        def warm(i):
+            warm_bank = psum.tile([P, N_BANK], F32, name="acc%d" % (PSUM_BANKS - 1))
+            for k in range(WARM_PER_CHUNK):
+                nc.tensor.matmul(
+                    out=warm_bank[:, 0:WARM_COLS],
+                    lhsT=x_raw[(0, 0)][:, 0, 0:P],
+                    rhs=g_raw[i][:, k, 0:WARM_COLS],
+                    start=True,
+                    stop=True,
+                )
+
         def empty_bank(n):
             t, eb = divmod(n, BANKS)
             h, k = divmod(eb, HALF)
@@ -214,7 +229,7 @@ def tile_featureembed_kernel(tc, x, mask, W, b, grad_out, out):
             cuts = STORE_CUTS.get(u, (0, HALF))
             if k + 1 in cuts:
                 k0 = cuts[cuts.index(k + 1) - 1]
-                queue = nc.scalar if h == 0 else nc.sync
+                queue = nc.scalar if n % 2 == 0 else nc.sync
                 queue.dma_start(
                     out=rows[:, k0 * N_BANK : (k + 1) * N_BANK], in_=ot[:, k0 * N_BANK : (k + 1) * N_BANK]
                 )
@@ -250,13 +265,15 @@ def tile_featureembed_kernel(tc, x, mask, W, b, grad_out, out):
                 quantise_g(i, 4)
                 quantise_g(i, 5)
             if i == HEAD_START_AFTER:
-                for n in range(PSUM_BANKS):
+                for n in range(HEAD_BANKS):
                     mx_pass(n, 0)
+            if i in WARM_CHUNKS:
+                warm(i)
 
         for n in range(total):
             mx_pass(n, 1)
             empty_bank(n)
-            if PSUM_BANKS <= n + AHEAD < total:
+            if HEAD_BANKS <= n + AHEAD < total:
                 mx_pass(n + AHEAD, 0)
             piece = n // (2 * BANKS) + 1
             if piece < G // XA:

@@ -25,10 +25,10 @@ E_MASK = E // NP
 XA = 256
 HALF = 3
 PSUM_BANKS = 8
-AHEAD = 4
+AHEAD = 1
 OUT_BUFS = 8
 X_PARTS = ((0, XA), (XA, G))
-STORE_CUTS = {0: (0, 1, 2, 3), 1: (0, 1, 2, 3), 15: (0, 1, 2, 3)}
+STORE_CUTS = {0: (0, 1, 3), 1: (0, 1, 3)}
 CHUNK_ORDER = ((0, 0, 4), (0, 4, 4), (0, 8, 4), (1, 0, 4), (0, 12, 4), (1, 4, 4), (1, 8, 4), (1, 12, 2), (1, 14, 2))
 N_CHUNKS = len(CHUNK_ORDER)
 HEAD_START_AFTER = 5
@@ -194,20 +194,6 @@ def tile_featureembed_kernel(tc, x, mask, W, b, grad_out, out):
             bank = accs[n][:].rearrange("q (p e) -> q e p", p=NP)
             e0 = eb * E_BANK
             rows = out[t * P : (t + 1) * P, h * HALF * N_BANK : (h + 1) * HALF * N_BANK]
-            if n == total - 1:
-                ew = E_BANK // 2
-                for part, queue in enumerate((nc.scalar, nc.sync)):
-                    c0 = k * N_BANK + part * ew * NP
-                    nc.vector.tensor_tensor(
-                        out=ot[:, c0 : c0 + ew * NP].rearrange("q (e p) -> q e p", p=NP),
-                        in0=bank[:, part * ew : (part + 1) * ew, :],
-                        in1=mask_e[t // 2][:, t % 2, e0 + part * ew : e0 + (part + 1) * ew]
-                        .unsqueeze(2)
-                        .to_broadcast([P, ew, NP]),
-                        op=MULT,
-                    )
-                    queue.dma_start(out=rows[:, c0 : c0 + ew * NP], in_=ot[:, c0 : c0 + ew * NP])
-                return
             if n % 2 == 1:
                 nc.vector.tensor_tensor(
                     out=ot[:, k * N_BANK : (k + 1) * N_BANK].rearrange("q (e p) -> q e p", p=NP),

@@ -142,7 +142,10 @@ def tile_featureembed_kernel(tc, x, mask, W, b, grad_out, out):
                     in_=src.rearrange("q j p (n i) -> q p n j i", i=4),
                 )
             else:
-                nc.scalar.copy(out=dst, in_=src.rearrange("q j p e -> q p e j"))
+                nc.scalar.copy(
+                    out=dst.rearrange("q p (n i) j -> q p n j i", i=4),
+                    in_=src.rearrange("q j p (n i) -> q p n j i", i=4),
+                )
 
         def quantise_g(i, eb):
             c, p0, pn = CHUNK_ORDER[i]

@@ -27,6 +27,7 @@ HALF = 3
 PSUM_BANKS = 8
 AHEAD = 1
 OUT_BUFS = 8
+DMA_ALIGN = 512
 X_PARTS = ((0, XA), (XA, G))
 STORE_CUTS = {0: (0, 1, 3), 1: (0, 1, 3)}
 CHUNK_ORDER = ((0, 0, 4), (0, 4, 4), (0, 8, 4), (1, 0, 4), (0, 12, 4), (1, 4, 4), (1, 8, 4), (1, 12, 2), (1, 14, 2))
@@ -66,11 +67,11 @@ def tile_featureembed_kernel(tc, x, mask, W, b, grad_out, out):
         x_raw = {}
         for c in range(PASSES):
             for g0, g1 in X_PARTS:
-                xr = raw.tile([P, PACK, g1 - g0], BF16, name="x_raw%d_%d" % (c, g0))
+                xr = raw.tile([P, PACK, g1 - g0], BF16, name="x_raw%d_%d" % (c, g0), align_bytes=DMA_ALIGN)
                 x_raw[(c, g0)] = xr
         g_raw = []
         for i in range(N_CHUNKS):
-            gr = raw.tile([P, PACK, CHUNK_ORDER[i][2] * E], BF16, name="g_raw%d" % i)
+            gr = raw.tile([P, PACK, CHUNK_ORDER[i][2] * E], BF16, name="g_raw%d" % i, align_bytes=DMA_ALIGN)
             g_raw.append(gr)
 
         def load_x(c, g0, g1):
@@ -191,7 +192,7 @@ def tile_featureembed_kernel(tc, x, mask, W, b, grad_out, out):
             h, k = divmod(eb, HALF)
             u = t * (BANKS // HALF) + h
             if k == 0:
-                ot = outp.tile([P, HALF * N_BANK], F32, name="ot%d" % (u % OUT_BUFS))
+                ot = outp.tile([P, HALF * N_BANK], F32, name="ot%d" % (u % OUT_BUFS), align_bytes=DMA_ALIGN)
                 outs[u] = ot
             ot = outs[u]
             bank = accs[n][:].rearrange("q (p e) -> q e p", p=NP)

from contextlib import ExitStack

import concourse.mybir as mybir

F32 = mybir.dt.float32
BF16 = mybir.dt.bfloat16
U32 = mybir.dt.uint32
U8 = mybir.dt.uint8
E4X4 = mybir.dt.float8_e4m3fn_x4
E5X4 = mybir.dt.float8_e5m2_x4
COPY = mybir.ActivationFunctionType.Copy
MULT = mybir.AluOpType.mult

C, G, NP, E = 1024, 1024, 16, 192
J = NP * E
P = 128
PACK = 4
K_PASS = P * PACK
PASSES = C // K_PASS
N_BANK = 512
E_BANK = N_BANK // NP
BANKS = J // N_BANK
G_TILES = G // P
E_MASK = E // NP
XA = 256
HALF = 3
PSUM_BANKS = 8
AHEAD = 1
OUT_BUFS = 8
DMA_ALIGN = 512
X_PARTS = ((0, XA), (XA, G))
STORE_CUTS = {0: (0, 1, 3), 1: (0, 1, 3)}
CHUNK_ORDER = ((0, 0, 4), (0, 4, 4), (0, 8, 4), (1, 0, 4), (0, 12, 4), (1, 4, 4), (1, 8, 4), (1, 12, 2), (1, 14, 2))
N_CHUNKS = len(CHUNK_ORDER)
HEAD_START_AFTER = 5
HEAD_BANKS = PSUM_BANKS - 1
WARM_CHUNKS = (6, 7)
WARM_PER_CHUNK = 3
WARM_COLS = 2 * E

FLOPS = 2 * C * G * J
BYTES = 2 * C * G + 2 * C * J + 2 * G * NP + 4 * G * J


def tile_featureembed_kernel(tc, x, mask, W, b, grad_out, out):
    nc = tc.nc
    with ExitStack() as ctx:
        raw = ctx.enter_context(tc.tile_pool(name="raw", bufs=1))
        keep = ctx.enter_context(tc.tile_pool(name="keep", bufs=1))
        grp = ctx.enter_context(tc.tile_pool(name="grp", bufs=1))
        outp = ctx.enter_context(tc.tile_pool(name="outp", bufs=1))
        psum = ctx.enter_context(tc.psum_pool(name="psum", bufs=1))
        ctx.enter_context(tc.manual_schedule())

        x_codes = keep.tile([P, PASSES, G], U32, align_bytes=64)
        x_scales = keep.tile([P, PASSES, G], U8, align_bytes=64)
        g_codes = keep.tile([P, PASSES, J], U32, align_bytes=64)
        g_scales = keep.tile([P, PASSES, J], U8, align_bytes=64)
        mask_bf = []
        mask_e = []
        for u in range(G // XA):
            mb = keep.tile([P, XA // P, NP], BF16, name="mask_bf%d" % u)
            me = keep.tile([P, XA // P, E], F32, name="mask_e%d" % u)
            mask_bf.append(mb)
            mask_e.append(me)

        x_raw = {}
        for c in range(PASSES):
            for g0, g1 in X_PARTS:
                xr = raw.tile([P, PACK, g1 - g0], BF16, name="x_raw%d_%d" % (c, g0), align_bytes=DMA_ALIGN)
                x_raw[(c, g0)] = xr
        g_raw = []
        for i in range(N_CHUNKS):
            gr = raw.tile([P, PACK, CHUNK_ORDER[i][2] * E], BF16, name="g_raw%d" % i, align_bytes=DMA_ALIGN)
            g_raw.append(gr)

        def load_x(c, g0, g1):
            rows = x[c * K_PASS : (c + 1) * K_PASS, g0:g1]
            nc.sync.dma_start(out=x_raw[(c, g0)][:], in_=rows.rearrange("(q j) g -> q j g", j=PACK))

        def load_mask(u):
            rows = mask[u * XA : (u + 1) * XA, :]
            nc.sync.dma_start(out=mask_bf[u][:], in_=rows.rearrange("(t q) m -> q t m", q=P))

        def expand_mask(u):
            nc.scalar.copy(
                out=mask_e[u][:].rearrange("q t (m r) -> q (t m) r", r=E_MASK),
                in_=mask_bf[u][:]
                .rearrange("q t m -> q (t m)")
                .unsqueeze(2)
                .to_broadcast([P, XA // P * NP, E_MASK]),
            )

        for i in range(N_CHUNKS):
            c, p0, pn = CHUNK_ORDER[i]
            rows = grad_out[c * K_PASS : (c + 1) * K_PASS, p0 : p0 + pn, :]
            nc.sync.dma_start(out=g_raw[i][:], in_=rows.rearrange("(q j) p e -> q j (p e)", j=PACK))
            if i == 0:
                load_mask(0)
                for c in range(PASSES):
                    load_x(c, 0, XA)
        load_x(0, XA, G)
        for u in range(1, G // XA):
            load_mask(u)
        load_x(1, XA, G)

        expand_mask(0)

        xgs = {}

        def copy_x(c, piece):
            g0 = piece * XA
            xg = grp.tile([P, XA, PACK], BF16, name="xg%d" % ((2 * piece + c) % 4), align_bytes=64)
            xgs[(c, piece)] = xg
            base = 0 if piece == 0 else XA
            part = x_raw[(c, base)]
            nc.vector.tensor_copy(
                out=xg[:].rearrange("q (n i) j -> q n j i", i=4),
                in_=part[:, :, g0 - base : g0 - base + XA].rearrange("q j (n i) -> q n j i", i=4),
            )

        def quantise_x(c, piece):
            g0 = piece * XA
            nc.vector.quantize_mx(
                out=x_codes[:, c, g0 : g0 + XA].bitcast(E4X4),
                scales=x_scales[:, c, g0 : g0 + XA],
                in_=xgs[(c, piece)][:].rearrange("q g j -> q (g j)"),
            )

        ggs = {}

        def copy_g(i, eb):
            pn = CHUNK_ORDER[i][2]
            if i not in ggs:
                gg = grp.tile([P, BANKS, pn, E_BANK, PACK], BF16, name="gg%d" % i, align_bytes=64)
                ggs[i] = gg
            rows = g_raw[i][:].rearrange("q j (p e) -> q j p e", p=pn)
            src = rows[:, :, :, eb * E_BANK : (eb + 1) * E_BANK]
            dst = ggs[i][:, eb, :, :, :]
            if eb % 2 == 0:
                nc.vector.tensor_copy(
                    out=dst.rearrange("q p (n i) j -> q p n j i", i=4),
                    in_=src.rearrange("q j p (n i) -> q p n j i", i=4),
                )
            else:
                nc.scalar.copy(
                    out=dst.rearrange("q p (n i) j -> q p n j i", i=4),
                    in_=src.rearrange("q j p (n i) -> q p n j i", i=4),
                )

        def quantise_g(i, eb):
            c, p0, pn = CHUNK_ORDER[i]
            c0 = eb * N_BANK + p0 * E_BANK
            nc.vector.quantize_mx(
                out=g_codes[:, c, c0 : c0 + pn * E_BANK].bitcast(E5X4),
                scales=g_scales[:, c, c0 : c0 + pn * E_BANK],
                in_=ggs[i][:, eb, :, :, :].rearrange("q p e j -> q (p e j)"),
            )

        accs = {}
        outs = {}
        total = G_TILES * BANKS

        def mx_pass(n, c):
            t, eb = divmod(n, BANKS)
            if c == 0:
                acc = psum.tile([P, N_BANK], F32, name="acc%d" % (n % PSUM_BANKS))
                accs[n] = acc
            nc.tensor.matmul_mx(
                out=accs[n][:],
                lhsT=x_codes[:, c, t * P : (t + 1) * P].bitcast(E4X4),
                lhsT_scale=x_scales[:, c, t * P : (t + 1) * P],
                rhs=g_codes[:, c, eb * N_BANK : (eb + 1) * N_BANK].bitcast(E5X4),
                rhs_scale=g_scales[:, c, eb * N_BANK : (eb + 1) * N_BANK],
                start=(c == 0),
                stop=(c == PASSES - 1),
            )

        def warm(i):
            warm_bank = psum.tile([P, N_BANK], F32, name="acc%d" % (PSUM_BANKS - 1))
            for k in range(WARM_PER_CHUNK):
                nc.tensor.matmul(
                    out=warm_bank[:, 0:WARM_COLS],
                    lhsT=x_raw[(0, 0)][:, 0, 0:P],
                    rhs=g_raw[i][:, k, 0:WARM_COLS],
                    start=True,
                    stop=True,
                )

        def empty_bank(n):
            t, eb = divmod(n, BANKS)
            h, k = divmod(eb, HALF)
            u = t * (BANKS // HALF) + h
            if k == 0:
                ot = outp.tile([P, HALF * N_BANK], F32, name="ot%d" % (u % OUT_BUFS), align_bytes=DMA_ALIGN)
                outs[u] = ot
            ot = outs[u]
            bank = accs[n][:].rearrange("q (p e) -> q e p", p=NP)
            e0 = eb * E_BANK
            rows = out[t * P : (t + 1) * P, h * HALF * N_BANK : (h + 1) * HALF * N_BANK]
            if n % 2 == 1:
                nc.vector.tensor_tensor(
                    out=ot[:, k * N_BANK : (k + 1) * N_BANK].rearrange("q (e p) -> q e p", p=NP),
                    in0=bank,
                    in1=mask_e[t // 2][:, t % 2, e0 : e0 + E_BANK].unsqueeze(2).to_broadcast([P, E_BANK, NP]),
                    op=MULT,
                )
            else:
                for m in range(e0 // E_MASK, (e0 + E_BANK - 1) // E_MASK + 1):
                    ea = max(e0, m * E_MASK)
                    ez = min(e0 + E_BANK, (m + 1) * E_MASK)
                    dst = ot[:, (ea - h * HALF * E_BANK) * NP : (ez - h * HALF * E_BANK) * NP]
                    nc.scalar.activation(
                        out=dst.rearrange("q (e p) -> q e p", p=NP),
                        in_=bank[:, ea - e0 : ez - e0, :],
                        func=COPY,
                        scale=mask_e[t // 2][:, t % 2, m * E_MASK : m * E_MASK + 1],
                    )
            cuts = STORE_CUTS.get(u, (0, HALF))
            if k + 1 in cuts:
                k0 = cuts[cuts.index(k + 1) - 1]
                queue = nc.scalar if n % 2 == 0 else nc.sync
                queue.dma_start(
                    out=rows[:, k0 * N_BANK : (k + 1) * N_BANK], in_=ot[:, k0 * N_BANK : (k + 1) * N_BANK]
                )

        last = N_CHUNKS - 1
        for i in range(last + 1):
            for eb in (1, 3, 5):
                copy_g(i, eb)
            if i < last:
                for eb in (0, 2, 4):
                    copy_g(i, eb)
                    if i > 0:
                        quantise_g(i - 1, eb + 1)
                if i == 0:
                    copy_x(0, 0)
                    copy_x(1, 0)
                for eb in (0, 2, 4):
                    quantise_g(i, eb)
                if i == 0:
                    quantise_x(0, 0)
                    quantise_x(1, 0)
            else:
                copy_g(i, 0)
                quantise_g(i - 1, 1)
                quantise_g(i, 0)
                copy_g(i, 2)
                quantise_g(i, 1)
                quantise_g(i - 1, 3)
                quantise_g(i, 2)
                copy_g(i, 4)
                quantise_g(i, 3)
                quantise_g(i - 1, 5)
                quantise_g(i, 4)
                quantise_g(i, 5)
            if i == HEAD_START_AFTER:
                for n in range(HEAD_BANKS):
                    mx_pass(n, 0)
            if i in WARM_CHUNKS:
                warm(i)

        for n in range(total):
            mx_pass(n, 1)
            empty_bank(n)
            if HEAD_BANKS <= n + AHEAD < total:
                mx_pass(n + AHEAD, 0)
            piece = n // (2 * BANKS) + 1
            if piece < G // XA:
                if n % (2 * BANKS) == 9:
                    expand_mask(piece)
                if n % (2 * BANKS) == 3:
                    copy_x(0, piece)
                if n % (2 * BANKS) == 5:
                    quantise_x(0, piece)
                if n % (2 * BANKS) == 7:
                    copy_x(1, piece)
                if n % (2 * BANKS) == 9:
                    quantise_x(1, piece)
